import numpy as np
import ml_dtypes

BF16 = ml_dtypes.bfloat16


def bf(x):
    return np.asarray(x, np.float32).astype(BF16)


def f32(x):
    return np.asarray(x, np.float32)


def f64(x):
    return np.asarray(x).astype(np.float64)


def striped(idx):
    return np.tile(idx.reshape(-1, 16).T, (8, 1))


S, D, H, P, N = 512, 128, 128, 384, 128


def silu(v):
    return v / (1.0 + np.exp(-v))


def setup_inputs():
    return {"table": bf(np.random.standard_normal((S, D))), "w1": bf(np.random.standard_normal((D, H)) / np.sqrt(D)), "b1": f32(0.1 * np.random.standard_normal((H, 1))), "w2": bf(np.random.standard_normal((H, P)) / np.sqrt(H)), "b2": f32(0.1 * np.random.standard_normal((P, 1))), "offs": striped(np.random.permutation(np.tile(np.arange(S), 2))[:N])}


def reference(table, w1, b1, w2, b2, offs):
    idx = offs[:16].T.reshape(-1)
    s = f64(table)[idx].T
    hid = silu(f64(w1).T @ s + f64(b1))
    phi = f64(w2).T @ hid + f64(b2)
    return np.concatenate([s, phi], axis=0)

@@ -1,0 +1,62 @@
+import concourse.mybir as mybir
+from concourse.masks import make_identity
+
+P = 128
+TYPES = 512
+TYPE_BLOCKS = TYPES // P
+ATOMS = 128
+OUT_BLOCKS = 3
+
+BF16, F32, U16 = mybir.dt.bfloat16, mybir.dt.float32, mybir.dt.uint16
+
+FLOPS = 2 * P * P * ATOMS + 2 * P * OUT_BLOCKS * P * ATOMS
+
+
+def tile_painn_kernel(tc, table, w1, b1, w2, b2, offs, out):
+    nc = tc.nc
+    with (
+        tc.tile_pool(name="held", bufs=1) as held,
+        tc.psum_pool(name="psum", bufs=1) as psum,
+    ):
+        rows = held.tile([P, TYPE_BLOCKS, P], BF16, name="rows")
+        nc.sync.dma_start(rows[:], table.rearrange("(b p) d -> p b d", p=P))
+        offsets = held.tile([P, ATOMS // 16], U16, name="offsets")
+        nc.sync.dma_start(offsets[:], offs)
+
+        w1_sb = held.tile([P, P], BF16, name="w1_sb")
+        nc.scalar.dma_start(w1_sb[:], w1)
+        b1_sb = held.tile([P, 1], F32, name="b1_sb")
+        nc.scalar.dma_start(b1_sb[:], b1)
+        w2_sb = held.tile([P, OUT_BLOCKS * P], BF16, name="w2_sb")
+        nc.scalar.dma_start(w2_sb[:], w2)
+        b2_sb = held.tile([P, OUT_BLOCKS], F32, name="b2_sb")
+        with nc.allow_non_contiguous_dma(reason="384 biases, one to a partition and block"):
+            nc.scalar.dma_start(b2_sb[:], b2.rearrange("(m p) o -> p (m o)", p=P))
+
+        identity = held.tile([P, P], BF16, name="identity")
+        make_identity(nc, identity[:])
+
+        flipped = psum.tile([P, TYPES], BF16, name="flipped")
+        for b in range(TYPE_BLOCKS):
+            nc.tensor.transpose(flipped[:, b * P : (b + 1) * P], rows[:, b, :], identity[:])
+        window = held.tile([P, TYPES], BF16, name="window")
+        nc.vector.tensor_copy(window[:], flipped[:])
+
+        hid_ps = psum.tile([P, ATOMS], F32, name="hid_ps")
+        nc.tensor.matmul(hid_ps[:], w1_sb[:], window[:].indirect(offsets[:]), start=True, stop=True)
+        emb_ps = psum.tile([P, ATOMS], F32, name="emb_ps")
+        nc.tensor.matmul(emb_ps[:], identity[:], window[:].indirect(offsets[:]), start=True, stop=True)
+
+        hid = held.tile([P, ATOMS], BF16, name="hid")
+        nc.scalar.activation(hid[:], hid_ps[:], mybir.ActivationFunctionType.Silu, bias=b1_sb[:])
+
+        emb = held.tile([P, ATOMS], F32, name="emb")
+        nc.vector.tensor_copy(emb[:], emb_ps[:])
+        nc.sync.dma_start(out[0:P, :], emb[:])
+
+        for m in range(OUT_BLOCKS):
+            phi_ps = psum.tile([P, ATOMS], F32, name=f"phi_ps{m}")
+            nc.tensor.matmul(phi_ps[:], w2_sb[:, m * P : (m + 1) * P], hid[:], start=True, stop=True)
+            phi = held.tile([P, ATOMS], F32, name=f"phi{m}")
+            nc.vector.tensor_scalar_add(phi[:], phi_ps[:], b2_sb[:, m : m + 1])
+            nc.sync.dma_start(out[(m + 1) * P : (m + 2) * P, :], phi[:])

@@ -8,6 +8,7 @@ ATOMS = 128
 OUT_BLOCKS = 3
 
 BF16, F32, U16 = mybir.dt.bfloat16, mybir.dt.float32, mybir.dt.uint16
+SILU = mybir.ActivationFunctionType.Silu
 
 FLOPS = 2 * P * P * ATOMS + 2 * P * OUT_BLOCKS * P * ATOMS
 
@@ -18,29 +19,39 @@ def tile_painn_kernel(tc, table, w1, b1, w2, b2, offs, out):
         tc.tile_pool(name="held", bufs=1) as held,
         tc.psum_pool(name="psum", bufs=1) as psum,
     ):
-        rows = held.tile([P, TYPE_BLOCKS, P], BF16, name="rows")
-        nc.sync.dma_start(rows[:], table.rearrange("(b p) d -> p b d", p=P))
+        rows = []
+        for b in range(TYPE_BLOCKS):
+            rows.append(held.tile([P, P], BF16, name=f"rows{b}"))
+            nc.sync.dma_start(rows[b][:], table[b * P : (b + 1) * P, :])
         offsets = held.tile([P, ATOMS // 16], U16, name="offsets")
         nc.sync.dma_start(offsets[:], offs)
+        b1_sb = held.tile([P, 1], F32, name="b1_sb")
+        nc.sync.dma_start(b1_sb[:], b1)
+        b2_sb = held.tile([P, OUT_BLOCKS], F32, name="b2_sb")
+        with nc.allow_non_contiguous_dma(reason="384 biases, one to a partition and block"):
+            nc.sync.dma_start(b2_sb[:], b2.rearrange("(m p) o -> p (m o)", p=P))
 
         w1_sb = held.tile([P, P], BF16, name="w1_sb")
         nc.scalar.dma_start(w1_sb[:], w1)
-        b1_sb = held.tile([P, 1], F32, name="b1_sb")
-        nc.scalar.dma_start(b1_sb[:], b1)
-        w2_sb = held.tile([P, OUT_BLOCKS * P], BF16, name="w2_sb")
-        nc.scalar.dma_start(w2_sb[:], w2)
-        b2_sb = held.tile([P, OUT_BLOCKS], F32, name="b2_sb")
-        with nc.allow_non_contiguous_dma(reason="384 biases, one to a partition and block"):
-            nc.scalar.dma_start(b2_sb[:], b2.rearrange("(m p) o -> p (m o)", p=P))
 
         identity = held.tile([P, P], BF16, name="identity")
         make_identity(nc, identity[:])
+        w2_sb = held.tile([P, OUT_BLOCKS * P], BF16, name="w2_sb")
+        nc.gpsimd.dma_start(w2_sb[:], w2)
 
-        flipped = psum.tile([P, TYPES], BF16, name="flipped")
-        for b in range(TYPE_BLOCKS):
-            nc.tensor.transpose(flipped[:, b * P : (b + 1) * P], rows[:, b, :], identity[:])
+        zero = held.tile([P, 1], F32, name="zero")
+        nc.vector.memset(zero[:], 0.0)
+        warmed = held.tile([P, 1], F32, name="warmed")
+        nc.scalar.activation(warmed[:], zero[:], SILU)
+
         window = held.tile([P, TYPES], BF16, name="window")
-        nc.vector.tensor_copy(window[:], flipped[:])
+        for b in range(TYPE_BLOCKS):
+            flipped = psum.tile([P, P], BF16, name=f"flipped{b}")
+            nc.tensor.transpose(flipped[:], rows[b][:], identity[:])
+            if b % 2 == 0:
+                nc.vector.tensor_copy(window[:, b * P : (b + 1) * P], flipped[:])
+            else:
+                nc.scalar.copy(window[:, b * P : (b + 1) * P], flipped[:])
 
         hid_ps = psum.tile([P, ATOMS], F32, name="hid_ps")
         nc.tensor.matmul(hid_ps[:], w1_sb[:], window[:].indirect(offsets[:]), start=True, stop=True)
@@ -48,15 +59,15 @@ def tile_painn_kernel(tc, table, w1, b1, w2, b2, offs, out):
         nc.tensor.matmul(emb_ps[:], identity[:], window[:].indirect(offsets[:]), start=True, stop=True)
 
         hid = held.tile([P, ATOMS], BF16, name="hid")
-        nc.scalar.activation(hid[:], hid_ps[:], mybir.ActivationFunctionType.Silu, bias=b1_sb[:])
+        nc.scalar.activation(hid[:], hid_ps[:], SILU, bias=b1_sb[:])
 
         emb = held.tile([P, ATOMS], F32, name="emb")
         nc.vector.tensor_copy(emb[:], emb_ps[:])
         nc.sync.dma_start(out[0:P, :], emb[:])
 
+        phi_ps = psum.tile([P, OUT_BLOCKS, ATOMS], F32, name="phi_ps")
         for m in range(OUT_BLOCKS):
-            phi_ps = psum.tile([P, ATOMS], F32, name=f"phi_ps{m}")
-            nc.tensor.matmul(phi_ps[:], w2_sb[:, m * P : (m + 1) * P], hid[:], start=True, stop=True)
+            nc.tensor.matmul(phi_ps[:, m, :], w2_sb[:, m * P : (m + 1) * P], hid[:], start=True, stop=True)
             phi = held.tile([P, ATOMS], F32, name=f"phi{m}")
-            nc.vector.tensor_scalar_add(phi[:], phi_ps[:], b2_sb[:, m : m + 1])
+            nc.vector.tensor_scalar_add(phi[:], phi_ps[:, m, :], b2_sb[:, m : m + 1])
             nc.sync.dma_start(out[(m + 1) * P : (m + 2) * P, :], phi[:])

@@ -9,6 +9,7 @@ OUT_BLOCKS = 3
 
 BF16, F32, U16 = mybir.dt.bfloat16, mybir.dt.float32, mybir.dt.uint16
 SILU = mybir.ActivationFunctionType.Silu
+IDENTITY = mybir.ActivationFunctionType.Identity
 
 FLOPS = 2 * P * P * ATOMS + 2 * P * OUT_BLOCKS * P * ATOMS
 
@@ -18,6 +19,7 @@ def tile_painn_kernel(tc, table, w1, b1, w2, b2, offs, out):
     with (
         tc.tile_pool(name="held", bufs=1) as held,
         tc.psum_pool(name="psum", bufs=1) as psum,
+        tc.psum_pool(name="phi_banks", bufs=2) as phi_banks,
     ):
         rows = []
         for b in range(TYPE_BLOCKS):
@@ -33,11 +35,11 @@ def tile_painn_kernel(tc, table, w1, b1, w2, b2, offs, out):
 
         w1_sb = held.tile([P, P], BF16, name="w1_sb")
         nc.scalar.dma_start(w1_sb[:], w1)
+        w2_sb = held.tile([P, OUT_BLOCKS * P], BF16, name="w2_sb")
+        nc.scalar.dma_start(w2_sb[:], w2)
 
         identity = held.tile([P, P], BF16, name="identity")
         make_identity(nc, identity[:])
-        w2_sb = held.tile([P, OUT_BLOCKS * P], BF16, name="w2_sb")
-        nc.gpsimd.dma_start(w2_sb[:], w2)
 
         zero = held.tile([P, 1], F32, name="zero")
         nc.vector.memset(zero[:], 0.0)
@@ -49,9 +51,9 @@ def tile_painn_kernel(tc, table, w1, b1, w2, b2, offs, out):
             flipped = psum.tile([P, P], BF16, name=f"flipped{b}")
             nc.tensor.transpose(flipped[:], rows[b][:], identity[:])
             if b % 2 == 0:
-                nc.vector.tensor_copy(window[:, b * P : (b + 1) * P], flipped[:])
-            else:
                 nc.scalar.copy(window[:, b * P : (b + 1) * P], flipped[:])
+            else:
+                nc.vector.tensor_copy(window[:, b * P : (b + 1) * P], flipped[:])
 
         hid_ps = psum.tile([P, ATOMS], F32, name="hid_ps")
         nc.tensor.matmul(hid_ps[:], w1_sb[:], window[:].indirect(offsets[:]), start=True, stop=True)
@@ -65,9 +67,13 @@ def tile_painn_kernel(tc, table, w1, b1, w2, b2, offs, out):
         nc.vector.tensor_copy(emb[:], emb_ps[:])
         nc.sync.dma_start(out[0:P, :], emb[:])
 
-        phi_ps = psum.tile([P, OUT_BLOCKS, ATOMS], F32, name="phi_ps")
         for m in range(OUT_BLOCKS):
-            nc.tensor.matmul(phi_ps[:, m, :], w2_sb[:, m * P : (m + 1) * P], hid[:], start=True, stop=True)
+            phi_ps = phi_banks.tile([P, ATOMS], F32, name="phi_ps")
+            nc.tensor.matmul(phi_ps[:], w2_sb[:, m * P : (m + 1) * P], hid[:], start=True, stop=True)
             phi = held.tile([P, ATOMS], F32, name=f"phi{m}")
-            nc.vector.tensor_scalar_add(phi[:], phi_ps[:, m, :], b2_sb[:, m : m + 1])
-            nc.sync.dma_start(out[(m + 1) * P : (m + 2) * P, :], phi[:])
+            if m % 2 == 0:
+                nc.vector.tensor_scalar_add(phi[:], phi_ps[:], b2_sb[:, m : m + 1])
+                nc.sync.dma_start(out[(m + 1) * P : (m + 2) * P, :], phi[:])
+            else:
+                nc.scalar.activation(phi[:], phi_ps[:], IDENTITY, bias=b2_sb[:, m : m + 1])
+                nc.scalar.dma_start(out[(m + 1) * P : (m + 2) * P, :], phi[:])

@@ -19,24 +19,23 @@ def tile_painn_kernel(tc, table, w1, b1, w2, b2, offs, out):
     with (
         tc.tile_pool(name="held", bufs=1) as held,
         tc.psum_pool(name="psum", bufs=1) as psum,
-        tc.psum_pool(name="phi_banks", bufs=2) as phi_banks,
     ):
-        rows = []
-        for b in range(TYPE_BLOCKS):
-            rows.append(held.tile([P, P], BF16, name=f"rows{b}"))
-            nc.sync.dma_start(rows[b][:], table[b * P : (b + 1) * P, :])
+        blocks = table.rearrange("(b p) d -> p b d", p=P)
+        rows = held.tile([P, TYPE_BLOCKS, P], BF16, name="rows")
+        nc.sync.dma_start(rows[:, 0:2, :], blocks[:, 0:2, :])
+        nc.scalar.dma_start(rows[:, 2:4, :], blocks[:, 2:4, :])
         offsets = held.tile([P, ATOMS // 16], U16, name="offsets")
         nc.sync.dma_start(offsets[:], offs)
-        b1_sb = held.tile([P, 1], F32, name="b1_sb")
-        nc.sync.dma_start(b1_sb[:], b1)
-        b2_sb = held.tile([P, OUT_BLOCKS], F32, name="b2_sb")
-        with nc.allow_non_contiguous_dma(reason="384 biases, one to a partition and block"):
-            nc.sync.dma_start(b2_sb[:], b2.rearrange("(m p) o -> p (m o)", p=P))
+        w2_sb = held.tile([P, OUT_BLOCKS * P], BF16, name="w2_sb")
+        nc.sync.dma_start(w2_sb[:], w2)
 
         w1_sb = held.tile([P, P], BF16, name="w1_sb")
         nc.scalar.dma_start(w1_sb[:], w1)
-        w2_sb = held.tile([P, OUT_BLOCKS * P], BF16, name="w2_sb")
-        nc.scalar.dma_start(w2_sb[:], w2)
+        b1_sb = held.tile([P, 1], F32, name="b1_sb")
+        nc.scalar.dma_start(b1_sb[:], b1)
+        b2_sb = held.tile([P, OUT_BLOCKS], F32, name="b2_sb")
+        with nc.allow_non_contiguous_dma(reason="384 biases, one to a partition and block"):
+            nc.scalar.dma_start(b2_sb[:], b2.rearrange("(m p) o -> p (m o)", p=P))
 
         identity = held.tile([P, P], BF16, name="identity")
         make_identity(nc, identity[:])
@@ -47,13 +46,11 @@ def tile_painn_kernel(tc, table, w1, b1, w2, b2, offs, out):
         nc.scalar.activation(warmed[:], zero[:], SILU)
 
         window = held.tile([P, TYPES], BF16, name="window")
-        for b in range(TYPE_BLOCKS):
-            flipped = psum.tile([P, P], BF16, name=f"flipped{b}")
-            nc.tensor.transpose(flipped[:], rows[b][:], identity[:])
-            if b % 2 == 0:
-                nc.scalar.copy(window[:, b * P : (b + 1) * P], flipped[:])
-            else:
-                nc.vector.tensor_copy(window[:, b * P : (b + 1) * P], flipped[:])
+        for half in range(2):
+            flipped = psum.tile([P, 2 * P], BF16, name=f"flipped{half}")
+            for side in range(2):
+                nc.tensor.transpose(flipped[:, side * P : (side + 1) * P], rows[:, 2 * half + side, :], identity[:])
+            nc.vector.tensor_copy(window[:, half * 2 * P : (half + 1) * 2 * P], flipped[:])
 
         hid_ps = psum.tile([P, ATOMS], F32, name="hid_ps")
         nc.tensor.matmul(hid_ps[:], w1_sb[:], window[:].indirect(offsets[:]), start=True, stop=True)
@@ -68,7 +65,7 @@ def tile_painn_kernel(tc, table, w1, b1, w2, b2, offs, out):
         nc.sync.dma_start(out[0:P, :], emb[:])
 
         for m in range(OUT_BLOCKS):
-            phi_ps = phi_banks.tile([P, ATOMS], F32, name="phi_ps")
+            phi_ps = psum.tile([P, ATOMS], F32, name=f"phi_ps{m}")
             nc.tensor.matmul(phi_ps[:], w2_sb[:, m * P : (m + 1) * P], hid[:], start=True, stop=True)
             phi = held.tile([P, ATOMS], F32, name=f"phi{m}")
             if m % 2 == 0:

@@ -26,6 +26,8 @@ def tile_painn_kernel(tc, table, w1, b1, w2, b2, offs, out):
         nc.scalar.dma_start(rows[:, 2:4, :], blocks[:, 2:4, :])
         offsets = held.tile([P, ATOMS // 16], U16, name="offsets")
         nc.sync.dma_start(offsets[:], offs)
+        b2_rows = held.tile([OUT_BLOCKS, P], F32, name="b2_rows")
+        nc.sync.dma_start(b2_rows[:], b2.rearrange("(m p) o -> m (p o)", p=P))
         w2_sb = held.tile([P, OUT_BLOCKS * P], BF16, name="w2_sb")
         nc.sync.dma_start(w2_sb[:], w2)
 
@@ -33,9 +35,6 @@ def tile_painn_kernel(tc, table, w1, b1, w2, b2, offs, out):
         nc.scalar.dma_start(w1_sb[:], w1)
         b1_sb = held.tile([P, 1], F32, name="b1_sb")
         nc.scalar.dma_start(b1_sb[:], b1)
-        b2_sb = held.tile([P, OUT_BLOCKS], F32, name="b2_sb")
-        with nc.allow_non_contiguous_dma(reason="384 biases, one to a partition and block"):
-            nc.scalar.dma_start(b2_sb[:], b2.rearrange("(m p) o -> p (m o)", p=P))
 
         identity = held.tile([P, P], BF16, name="identity")
         make_identity(nc, identity[:])
@@ -63,6 +62,13 @@ def tile_painn_kernel(tc, table, w1, b1, w2, b2, offs, out):
         emb = held.tile([P, ATOMS], F32, name="emb")
         nc.vector.tensor_copy(emb[:], emb_ps[:])
         nc.sync.dma_start(out[0:P, :], emb[:])
+
+        small_identity = held.tile([OUT_BLOCKS, OUT_BLOCKS], F32, name="small_identity")
+        nc.vector.tensor_copy(small_identity[:], identity[0:OUT_BLOCKS, 0:OUT_BLOCKS])
+        b2_ps = psum.tile([P, OUT_BLOCKS], F32, name="b2_ps")
+        nc.tensor.matmul(b2_ps[:], b2_rows[:], small_identity[:], start=True, stop=True)
+        b2_sb = held.tile([P, OUT_BLOCKS], F32, name="b2_sb")
+        nc.vector.tensor_copy(b2_sb[:], b2_ps[:])
 
         for m in range(OUT_BLOCKS):
             phi_ps = psum.tile([P, ATOMS], F32, name=f"phi_ps{m}")

@@ -5,6 +5,7 @@ P = 128
 TYPES = 512
 TYPE_BLOCKS = TYPES // P
 ATOMS = 128
+WARM_TURNS = 10
 OUT_BLOCKS = 3
 
 BF16, F32, U16 = mybir.dt.bfloat16, mybir.dt.float32, mybir.dt.uint16
@@ -39,10 +40,13 @@ def tile_painn_kernel(tc, table, w1, b1, w2, b2, offs, out):
         identity = held.tile([P, P], BF16, name="identity")
         make_identity(nc, identity[:])
 
-        zero = held.tile([P, 1], F32, name="zero")
-        nc.vector.memset(zero[:], 0.0)
+        zeros = held.tile([P, P], BF16, name="zeros")
+        nc.vector.memset(zeros[:], 0.0)
         warmed = held.tile([P, 1], F32, name="warmed")
-        nc.scalar.activation(warmed[:], zero[:], SILU)
+        nc.scalar.activation(warmed[:], zeros[:, 0:1], SILU)
+        hid_ps = psum.tile([P, ATOMS], F32, name="hid_ps")
+        for turn in range(WARM_TURNS):
+            nc.tensor.matmul(hid_ps[:], zeros[:], zeros[:], start=True, stop=True)
 
         window = held.tile([P, TYPES], BF16, name="window")
         for half in range(2):
@@ -51,7 +55,6 @@ def tile_painn_kernel(tc, table, w1, b1, w2, b2, offs, out):
                 nc.tensor.transpose(flipped[:, side * P : (side + 1) * P], rows[:, 2 * half + side, :], identity[:])
             nc.vector.tensor_copy(window[:, half * 2 * P : (half + 1) * 2 * P], flipped[:])
 
-        hid_ps = psum.tile([P, ATOMS], F32, name="hid_ps")
         nc.tensor.matmul(hid_ps[:], w1_sb[:], window[:].indirect(offsets[:]), start=True, stop=True)
         emb_ps = psum.tile([P, ATOMS], F32, name="emb_ps")
         nc.tensor.matmul(emb_ps[:], identity[:], window[:].indirect(offsets[:]), start=True, stop=True)

@@ -27,8 +27,8 @@ def tile_painn_kernel(tc, table, w1, b1, w2, b2, offs, out):
         nc.scalar.dma_start(rows[:, 2:4, :], blocks[:, 2:4, :])
         offsets = held.tile([P, ATOMS // 16], U16, name="offsets")
         nc.sync.dma_start(offsets[:], offs)
-        b2_rows = held.tile([OUT_BLOCKS, P], F32, name="b2_rows")
-        nc.sync.dma_start(b2_rows[:], b2.rearrange("(m p) o -> m (p o)", p=P))
+        b2_sb = held.tile([P, OUT_BLOCKS], F32, name="b2_sb")
+        nc.sync.dma_start(b2_sb[:], b2.rearrange("(p m) o -> p (m o)", m=OUT_BLOCKS))
         w2_sb = held.tile([P, OUT_BLOCKS * P], BF16, name="w2_sb")
         nc.sync.dma_start(w2_sb[:], w2)
 
@@ -66,20 +66,14 @@ def tile_painn_kernel(tc, table, w1, b1, w2, b2, offs, out):
         nc.vector.tensor_copy(emb[:], emb_ps[:])
         nc.sync.dma_start(out[0:P, :], emb[:])
 
-        small_identity = held.tile([OUT_BLOCKS, OUT_BLOCKS], F32, name="small_identity")
-        nc.vector.tensor_copy(small_identity[:], identity[0:OUT_BLOCKS, 0:OUT_BLOCKS])
-        b2_ps = psum.tile([P, OUT_BLOCKS], F32, name="b2_ps")
-        nc.tensor.matmul(b2_ps[:], b2_rows[:], small_identity[:], start=True, stop=True)
-        b2_sb = held.tile([P, OUT_BLOCKS], F32, name="b2_sb")
-        nc.vector.tensor_copy(b2_sb[:], b2_ps[:])
-
         for m in range(OUT_BLOCKS):
             phi_ps = psum.tile([P, ATOMS], F32, name=f"phi_ps{m}")
-            nc.tensor.matmul(phi_ps[:], w2_sb[:, m * P : (m + 1) * P], hid[:], start=True, stop=True)
+            nc.tensor.matmul(phi_ps[:], w2_sb[:, m : OUT_BLOCKS * P : OUT_BLOCKS], hid[:], start=True, stop=True)
             phi = held.tile([P, ATOMS], F32, name=f"phi{m}")
+            out_rows = out[P + m : (1 + OUT_BLOCKS) * P : OUT_BLOCKS, :]
             if m % 2 == 0:
                 nc.vector.tensor_scalar_add(phi[:], phi_ps[:], b2_sb[:, m : m + 1])
-                nc.sync.dma_start(out[(m + 1) * P : (m + 2) * P, :], phi[:])
+                nc.sync.dma_start(out_rows, phi[:])
             else:
                 nc.scalar.activation(phi[:], phi_ps[:], IDENTITY, bias=b2_sb[:, m : m + 1])
-                nc.scalar.dma_start(out[(m + 1) * P : (m + 2) * P, :], phi[:])
+                nc.scalar.dma_start(out_rows, phi[:])

@@ -27,10 +27,10 @@ def tile_painn_kernel(tc, table, w1, b1, w2, b2, offs, out):
         nc.scalar.dma_start(rows[:, 2:4, :], blocks[:, 2:4, :])
         offsets = held.tile([P, ATOMS // 16], U16, name="offsets")
         nc.sync.dma_start(offsets[:], offs)
-        b2_sb = held.tile([P, OUT_BLOCKS], F32, name="b2_sb")
-        nc.sync.dma_start(b2_sb[:], b2.rearrange("(p m) o -> p (m o)", m=OUT_BLOCKS))
         w2_sb = held.tile([P, OUT_BLOCKS * P], BF16, name="w2_sb")
         nc.sync.dma_start(w2_sb[:], w2)
+        b2_sb = held.tile([P, OUT_BLOCKS], F32, name="b2_sb")
+        nc.sync.dma_start(b2_sb[:], b2.rearrange("(p m) o -> p (m o)", m=OUT_BLOCKS))
 
         w1_sb = held.tile([P, P], BF16, name="w1_sb")
         nc.scalar.dma_start(w1_sb[:], w1)

@@ -49,11 +49,10 @@ def tile_painn_kernel(tc, table, w1, b1, w2, b2, offs, out):
             nc.tensor.matmul(hid_ps[:], zeros[:], zeros[:], start=True, stop=True)
 
         window = held.tile([P, TYPES], BF16, name="window")
-        for half in range(2):
-            flipped = psum.tile([P, 2 * P], BF16, name=f"flipped{half}")
-            for side in range(2):
-                nc.tensor.transpose(flipped[:, side * P : (side + 1) * P], rows[:, 2 * half + side, :], identity[:])
-            nc.vector.tensor_copy(window[:, half * 2 * P : (half + 1) * 2 * P], flipped[:])
+        for b in range(TYPE_BLOCKS):
+            flipped = psum.tile([P, P], BF16, name=f"flipped{b}", tag=f"bank{b}")
+            nc.tensor.transpose(flipped[:], rows[:, b, :], identity[:])
+            nc.vector.tensor_copy(window[:, b * P : (b + 1) * P], flipped[:])
 
         nc.tensor.matmul(hid_ps[:], w1_sb[:], window[:].indirect(offsets[:]), start=True, stop=True)
         emb_ps = psum.tile([P, ATOMS], F32, name="emb_ps")
@@ -67,7 +66,7 @@ def tile_painn_kernel(tc, table, w1, b1, w2, b2, offs, out):
         nc.sync.dma_start(out[0:P, :], emb[:])
 
         for m in range(OUT_BLOCKS):
-            phi_ps = psum.tile([P, ATOMS], F32, name=f"phi_ps{m}")
+            phi_ps = psum.tile([P, ATOMS], F32, name=f"phi_ps{m}", tag=f"bank{m}")
             nc.tensor.matmul(phi_ps[:], w2_sb[:, m : OUT_BLOCKS * P : OUT_BLOCKS], hid[:], start=True, stop=True)
             phi = held.tile([P, ATOMS], F32, name=f"phi{m}")
             out_rows = out[P + m : (1 + OUT_BLOCKS) * P : OUT_BLOCKS, :]

@@ -23,8 +23,9 @@ def tile_painn_kernel(tc, table, w1, b1, w2, b2, offs, out):
     ):
         blocks = table.rearrange("(b p) d -> p b d", p=P)
         rows = held.tile([P, TYPE_BLOCKS, P], BF16, name="rows")
-        nc.sync.dma_start(rows[:, 0:2, :], blocks[:, 0:2, :])
-        nc.scalar.dma_start(rows[:, 2:4, :], blocks[:, 2:4, :])
+        nc.sync.dma_start(rows[:, 0, :], blocks[:, 0, :])
+        nc.scalar.dma_start(rows[:, 1, :], blocks[:, 1, :])
+        nc.sync.dma_start(rows[:, 2:4, :], blocks[:, 2:4, :])
         offsets = held.tile([P, ATOMS // 16], U16, name="offsets")
         nc.sync.dma_start(offsets[:], offs)
         w2_sb = held.tile([P, OUT_BLOCKS * P], BF16, name="w2_sb")

@@ -5,7 +5,7 @@ P = 128
 TYPES = 512
 TYPE_BLOCKS = TYPES // P
 ATOMS = 128
-WARM_TURNS = 10
+WARM_TURNS = 9
 OUT_BLOCKS = 3
 
 BF16, F32, U16 = mybir.dt.bfloat16, mybir.dt.float32, mybir.dt.uint16

@@ -24,8 +24,8 @@ def tile_painn_kernel(tc, table, w1, b1, w2, b2, offs, out):
         blocks = table.rearrange("(b p) d -> p b d", p=P)
         rows = held.tile([P, TYPE_BLOCKS, P], BF16, name="rows")
         nc.sync.dma_start(rows[:, 0, :], blocks[:, 0, :])
-        nc.scalar.dma_start(rows[:, 1, :], blocks[:, 1, :])
-        nc.sync.dma_start(rows[:, 2:4, :], blocks[:, 2:4, :])
+        nc.scalar.dma_start(rows[:, 1:3, :], blocks[:, 1:3, :])
+        nc.sync.dma_start(rows[:, 3, :], blocks[:, 3, :])
         offsets = held.tile([P, ATOMS // 16], U16, name="offsets")
         nc.sync.dma_start(offsets[:], offs)
         w2_sb = held.tile([P, OUT_BLOCKS * P], BF16, name="w2_sb")

@@ -6,6 +6,7 @@ TYPES = 512
 TYPE_BLOCKS = TYPES // P
 ATOMS = 128
 WARM_TURNS = 9
+KEEP_TURNS = 3
 OUT_BLOCKS = 3
 
 BF16, F32, U16 = mybir.dt.bfloat16, mybir.dt.float32, mybir.dt.uint16
@@ -54,6 +55,8 @@ def tile_painn_kernel(tc, table, w1, b1, w2, b2, offs, out):
             flipped = psum.tile([P, P], BF16, name=f"flipped{b}", tag=f"bank{b}")
             nc.tensor.transpose(flipped[:], rows[:, b, :], identity[:])
             nc.vector.tensor_copy(window[:, b * P : (b + 1) * P], flipped[:])
+        for turn in range(KEEP_TURNS):
+            nc.tensor.matmul(hid_ps[:], identity[:], rows[:, TYPE_BLOCKS - 1, :], start=True, stop=True)
 
         nc.tensor.matmul(hid_ps[:], w1_sb[:], window[:].indirect(offsets[:]), start=True, stop=True)
         emb_ps = psum.tile([P, ATOMS], F32, name="emb_ps")

@@ -6,6 +6,7 @@ TYPES = 512
 TYPE_BLOCKS = TYPES // P
 ATOMS = 128
 WARM_TURNS = 9
+HALF = ATOMS // 2
 KEEP_TURNS = 3
 OUT_BLOCKS = 3
 
@@ -63,7 +64,9 @@ def tile_painn_kernel(tc, table, w1, b1, w2, b2, offs, out):
         nc.tensor.matmul(emb_ps[:], identity[:], window[:].indirect(offsets[:]), start=True, stop=True)
 
         hid = held.tile([P, ATOMS], BF16, name="hid")
-        nc.scalar.activation(hid[:], hid_ps[:], SILU, bias=b1_sb[:])
+        for first in range(0, ATOMS, HALF):
+            some = slice(first, first + HALF)
+            nc.scalar.activation(hid[:, some], hid_ps[:, some], SILU, bias=b1_sb[:])
 
         emb = held.tile([P, ATOMS], F32, name="emb")
         nc.vector.tensor_copy(emb[:], emb_ps[:])
@@ -71,7 +74,11 @@ def tile_painn_kernel(tc, table, w1, b1, w2, b2, offs, out):
 
         for m in range(OUT_BLOCKS):
             phi_ps = psum.tile([P, ATOMS], F32, name=f"phi_ps{m}", tag=f"bank{m}")
-            nc.tensor.matmul(phi_ps[:], w2_sb[:, m : OUT_BLOCKS * P : OUT_BLOCKS], hid[:], start=True, stop=True)
+            for first in range(0, ATOMS, HALF):
+                some = slice(first, first + HALF)
+                nc.tensor.matmul(
+                    phi_ps[:, some], w2_sb[:, m : OUT_BLOCKS * P : OUT_BLOCKS], hid[:, some], start=True, stop=True
+                )
             phi = held.tile([P, ATOMS], F32, name=f"phi{m}")
             out_rows = out[P + m : (1 + OUT_BLOCKS) * P : OUT_BLOCKS, :]
             if m % 2 == 0:

@@ -47,9 +47,10 @@ def tile_painn_kernel(tc, table, w1, b1, w2, b2, offs, out):
         nc.vector.memset(zeros[:], 0.0)
         warmed = held.tile([P, 1], F32, name="warmed")
         nc.scalar.activation(warmed[:], zeros[:, 0:1], SILU)
-        hid_ps = psum.tile([P, ATOMS], F32, name="hid_ps")
+        hid_ps = [psum.tile([P, HALF], F32, name=f"hid_ps{half}") for half in range(2)]
+        idle_ps = psum.tile([P, P], F32, name="idle_ps", tag="emb_ps")
         for turn in range(WARM_TURNS):
-            nc.tensor.matmul(hid_ps[:], zeros[:], zeros[:], start=True, stop=True)
+            nc.tensor.matmul(idle_ps[:], zeros[:], zeros[:], start=True, stop=True)
 
         window = held.tile([P, TYPES], BF16, name="window")
         for b in range(TYPE_BLOCKS):
@@ -57,16 +58,18 @@ def tile_painn_kernel(tc, table, w1, b1, w2, b2, offs, out):
             nc.tensor.transpose(flipped[:], rows[:, b, :], identity[:])
             nc.vector.tensor_copy(window[:, b * P : (b + 1) * P], flipped[:])
         for turn in range(KEEP_TURNS):
-            nc.tensor.matmul(hid_ps[:], identity[:], rows[:, TYPE_BLOCKS - 1, :], start=True, stop=True)
+            nc.tensor.matmul(idle_ps[:], identity[:], rows[:, TYPE_BLOCKS - 1, :], start=True, stop=True)
 
-        nc.tensor.matmul(hid_ps[:], w1_sb[:], window[:].indirect(offsets[:]), start=True, stop=True)
+        for half in range(2):
+            half_list = offsets[:, half * HALF // 16 : (half + 1) * HALF // 16]
+            nc.tensor.matmul(hid_ps[half][:], w1_sb[:], window[:].indirect(half_list), start=True, stop=True)
         emb_ps = psum.tile([P, ATOMS], F32, name="emb_ps")
         nc.tensor.matmul(emb_ps[:], identity[:], window[:].indirect(offsets[:]), start=True, stop=True)
 
         hid = held.tile([P, ATOMS], BF16, name="hid")
-        for first in range(0, ATOMS, HALF):
-            some = slice(first, first + HALF)
-            nc.scalar.activation(hid[:, some], hid_ps[:, some], SILU, bias=b1_sb[:])
+        for half in range(2):
+            some = slice(half * HALF, (half + 1) * HALF)
+            nc.scalar.activation(hid[:, some], hid_ps[half][:], SILU, bias=b1_sb[:])
 
         emb = held.tile([P, ATOMS], F32, name="emb")
         nc.vector.tensor_copy(emb[:], emb_ps[:])

@@ -5,7 +5,7 @@ P = 128
 TYPES = 512
 TYPE_BLOCKS = TYPES // P
 ATOMS = 128
-WARM_TURNS = 9
+WARM_TURNS = 12
 HALF = ATOMS // 2
 KEEP_TURNS = 3
 OUT_BLOCKS = 3

import concourse.mybir as mybir
from concourse.masks import make_identity

P = 128
TYPES = 512
TYPE_BLOCKS = TYPES // P
ATOMS = 128
WARM_TURNS = 12
HALF = ATOMS // 2
KEEP_TURNS = 3
OUT_BLOCKS = 3

BF16, F32, U16 = mybir.dt.bfloat16, mybir.dt.float32, mybir.dt.uint16
SILU = mybir.ActivationFunctionType.Silu
IDENTITY = mybir.ActivationFunctionType.Identity

FLOPS = 2 * P * P * ATOMS + 2 * P * OUT_BLOCKS * P * ATOMS


def tile_painn_kernel(tc, table, w1, b1, w2, b2, offs, out):
    nc = tc.nc
    with (
        tc.tile_pool(name="held", bufs=1) as held,
        tc.psum_pool(name="psum", bufs=1) as psum,
    ):
        blocks = table.rearrange("(b p) d -> p b d", p=P)
        rows = held.tile([P, TYPE_BLOCKS, P], BF16, name="rows")
        nc.sync.dma_start(rows[:, 0, :], blocks[:, 0, :])
        nc.scalar.dma_start(rows[:, 1:3, :], blocks[:, 1:3, :])
        nc.sync.dma_start(rows[:, 3, :], blocks[:, 3, :])
        offsets = held.tile([P, ATOMS // 16], U16, name="offsets")
        nc.sync.dma_start(offsets[:], offs)
        w2_sb = held.tile([P, OUT_BLOCKS * P], BF16, name="w2_sb")
        nc.sync.dma_start(w2_sb[:], w2)
        b2_sb = held.tile([P, OUT_BLOCKS], F32, name="b2_sb")
        nc.sync.dma_start(b2_sb[:], b2.rearrange("(p m) o -> p (m o)", m=OUT_BLOCKS))

        w1_sb = held.tile([P, P], BF16, name="w1_sb")
        nc.scalar.dma_start(w1_sb[:], w1)
        b1_sb = held.tile([P, 1], F32, name="b1_sb")
        nc.scalar.dma_start(b1_sb[:], b1)

        identity = held.tile([P, P], BF16, name="identity")
        make_identity(nc, identity[:])

        zeros = held.tile([P, P], BF16, name="zeros")
        nc.vector.memset(zeros[:], 0.0)
        warmed = held.tile([P, 1], F32, name="warmed")
        nc.scalar.activation(warmed[:], zeros[:, 0:1], SILU)
        hid_ps = [psum.tile([P, HALF], F32, name=f"hid_ps{half}") for half in range(2)]
        idle_ps = psum.tile([P, P], F32, name="idle_ps", tag="emb_ps")
        for turn in range(WARM_TURNS):
            nc.tensor.matmul(idle_ps[:], zeros[:], zeros[:], start=True, stop=True)

        window = held.tile([P, TYPES], BF16, name="window")
        for b in range(TYPE_BLOCKS):
            flipped = psum.tile([P, P], BF16, name=f"flipped{b}", tag=f"bank{b}")
            nc.tensor.transpose(flipped[:], rows[:, b, :], identity[:])
            nc.vector.tensor_copy(window[:, b * P : (b + 1) * P], flipped[:])
        for turn in range(KEEP_TURNS):
            nc.tensor.matmul(idle_ps[:], identity[:], rows[:, TYPE_BLOCKS - 1, :], start=True, stop=True)

        for half in range(2):
            half_list = offsets[:, half * HALF // 16 : (half + 1) * HALF // 16]
            nc.tensor.matmul(hid_ps[half][:], w1_sb[:], window[:].indirect(half_list), start=True, stop=True)
        emb_ps = psum.tile([P, ATOMS], F32, name="emb_ps")
        nc.tensor.matmul(emb_ps[:], identity[:], window[:].indirect(offsets[:]), start=True, stop=True)

        hid = held.tile([P, ATOMS], BF16, name="hid")
        for half in range(2):
            some = slice(half * HALF, (half + 1) * HALF)
            nc.scalar.activation(hid[:, some], hid_ps[half][:], SILU, bias=b1_sb[:])

        emb = held.tile([P, ATOMS], F32, name="emb")
        nc.vector.tensor_copy(emb[:], emb_ps[:])
        nc.sync.dma_start(out[0:P, :], emb[:])

        for m in range(OUT_BLOCKS):
            phi_ps = psum.tile([P, ATOMS], F32, name=f"phi_ps{m}", tag=f"bank{m}")
            for first in range(0, ATOMS, HALF):
                some = slice(first, first + HALF)
                nc.tensor.matmul(
                    phi_ps[:, some], w2_sb[:, m : OUT_BLOCKS * P : OUT_BLOCKS], hid[:, some], start=True, stop=True
                )
            phi = held.tile([P, ATOMS], F32, name=f"phi{m}")
            out_rows = out[P + m : (1 + OUT_BLOCKS) * P : OUT_BLOCKS, :]
            if m % 2 == 0:
                nc.vector.tensor_scalar_add(phi[:], phi_ps[:], b2_sb[:, m : m + 1])
                nc.sync.dma_start(out_rows, phi[:])
            else:
                nc.scalar.activation(phi[:], phi_ps[:], IDENTITY, bias=b2_sb[:, m : m + 1])
                nc.scalar.dma_start(out_rows, phi[:])
